import numpy as np
import ml_dtypes


def mxq(x, axis, fmt="e4m3"):
    dtype, down = {"e4m3": (ml_dtypes.float8_e4m3fn, 7), "e5m2": (ml_dtypes.float8_e5m2, 14)}[fmt]
    v = np.moveaxis(np.asarray(x, np.float32).astype(ml_dtypes.bfloat16).astype(np.float64), axis, -1)
    blocks = v.reshape(v.shape[:-1] + (-1, 32))
    amax = np.abs(blocks).max(-1, keepdims=True)
    byte = np.maximum(np.where(amax > 0, np.frexp(amax)[1] - 1 + 127, 0) - down, 1)
    scale = np.exp2(byte - 127.0)
    codes = (blocks / scale).astype(np.float32).astype(dtype).astype(np.float64)
    return np.moveaxis((codes * scale).reshape(v.shape), -1, axis)


WIDE = False


def mx_kscale(k):
    if not WIDE:
        return np.ones(k)
    levels = np.array([10, -10, 5, -5, 0])
    a = np.random.permutation(np.resize(levels, k // 512 * 4)).reshape(k // 512, 4)
    idx = np.arange(k)
    return np.exp2(a[idx // 512, idx % 128 // 32])


BF16 = ml_dtypes.bfloat16


def bf(x):
    return np.asarray(x, np.float32).astype(BF16)


def f64(x):
    return np.asarray(x).astype(np.float64)


I, B, D, H, F = 512, 2, 1024, 8, 128
EPS = 1e-5


def setup_inputs():
    s = mx_kscale(D)
    return {"x": bf(np.random.standard_normal((I, B, D))),
            "gamma": bf((1.0 + 0.1 * np.random.standard_normal(D)) * s),
            "beta": bf(0.1 * np.random.standard_normal(D) * s),
            "Wq": bf(np.random.standard_normal((D, H * F)) * 1.5 / np.sqrt(D) / s[:, None]),
            "Wv": bf(np.random.standard_normal((D, H * F)) * 1.5 / np.sqrt(D) / s[:, None]),
            "u_bias": bf(np.random.standard_normal((H, F)) * 0.5),
            "v_bias": bf(np.random.standard_normal((H, F)) * 0.5)}


def reference(x, gamma, beta, Wq, Wv, u_bias, v_bias):
    x = f64(x)
    mu = x.mean(-1, keepdims=True)
    var = ((x - mu) ** 2).mean(-1, keepdims=True)
    h = (x - mu) / np.sqrt(var + EPS) * f64(gamma) + f64(beta)
    hq = mxq(h, 2, "e4m3")
    q = (hq @ mxq(f64(Wq), 0, "e4m3")).reshape(I, B, H, F)
    v = (hq @ mxq(f64(Wv), 0, "e4m3")).reshape(I, B, H, F)
    return q + f64(u_bias), q + f64(v_bias), q, v

@@ -1,0 +1,270 @@
+from contextlib import ExitStack
+
+import concourse.mybir as mybir
+from concourse.masks import make_identity
+
+F32 = mybir.dt.float32
+BF16 = mybir.dt.bfloat16
+U32 = mybir.dt.uint32
+U8 = mybir.dt.uint8
+I32 = mybir.dt.int32
+FP8X4 = mybir.dt.float8_e4m3fn_x4
+ACT = mybir.ActivationFunctionType
+ALU = mybir.AluOpType
+
+P = 128
+PACK = 4
+K_PASS = P * PACK
+TOKENS = 1024
+D_MODEL = 1024
+FEATURES = 1024
+PASSES = D_MODEL // K_PASS
+CHUNKS = D_MODEL // P
+TOKEN_TILES = TOKENS // P
+GROUP = 2
+GROUPS = TOKEN_TILES // GROUP
+GROUP_TOKENS = GROUP * P
+N_TILE = 512
+HALVES = FEATURES // N_TILE
+HEADS = 8
+W_PIECE = 256
+BN_WIDTH = 512
+EPS = 1e-5
+
+FLOPS = 2 * TOKENS * D_MODEL * 2 * FEATURES
+
+
+def regroup_views(grouped, planes):
+    dst = grouped.rearrange("p (c i) t -> p c t i", i=4)
+    src = planes.rearrange("p t (c i) -> p c t i", i=4)
+    return dst, src
+
+
+def tile_multiheadattentiowithrpe_pa_kernel(
+    tc, x, gamma, beta, Wq, Wv, u_bias, v_bias, out_0, out_1, out_2, out_3
+):
+    nc = tc.nc
+
+    x_view = x.rearrange("i b d -> (i b) d").rearrange("(p j) d -> p j d", j=TOKEN_TILES)
+    out_views = [
+        o.rearrange("i b h f -> (i b) (h f)").rearrange("(p j) n -> p j n", j=TOKEN_TILES)
+        for o in (out_0, out_1, out_2, out_3)
+    ]
+    w_views = [w.rearrange("(g t p) n -> g p t n", t=PACK, p=P) for w in (Wq, Wv)]
+
+    with ExitStack() as ctx:
+        const = ctx.enter_context(tc.tile_pool(name="const", bufs=1))
+        keep = ctx.enter_context(tc.tile_pool(name="keep", bufs=1))
+        small = ctx.enter_context(tc.tile_pool(name="small", bufs=4))
+        work = ctx.enter_context(tc.tile_pool(name="work", bufs=2))
+        stage = ctx.enter_context(tc.tile_pool(name="stage", bufs=3))
+        psum_t = ctx.enter_context(tc.psum_pool(name="psum_t", bufs=3))
+        psum_o = ctx.enter_context(tc.psum_pool(name="psum_o", bufs=5))
+
+        ident = const.tile([P, P], F32, name="ident")
+        make_identity(nc, ident[:])
+        ident_bf = const.tile([P, P], BF16, name="ident_bf")
+        make_identity(nc, ident_bf[:])
+
+        rows = const.tile([P, P], BF16, name="rows")
+        nc.vector.memset(rows[:], 0.0)
+        for i, vec in enumerate(
+            (
+                gamma.rearrange("(c p) -> c p", p=P),
+                beta.rearrange("(c p) -> c p", p=P),
+                u_bias,
+                v_bias,
+            )
+        ):
+            nc.sync.dma_start(out=rows[i * CHUNKS : (i + 1) * CHUNKS, :], in_=vec)
+        eps = const.tile([P, 1], F32, name="eps")
+        nc.vector.memset(eps[:], EPS)
+        warm = const.tile([P, 1], F32, name="warm")
+        nc.scalar.activation(out=warm[:], in_=eps[:], func=ACT.Sqrt)
+
+        x_sb = [keep.tile([P, GROUP, D_MODEL], BF16, name="x_sb%d" % grp) for grp in range(GROUPS)]
+        w_raw = [
+            [keep.tile([P, PACK, FEATURES], BF16, name="w_raw%d%d" % (w, g)) for g in range(PASSES)]
+            for w in range(2)
+        ]
+
+        def load_x(grp):
+            nc.sync.dma_start(out=x_sb[grp][:], in_=x_view[:, grp * GROUP : (grp + 1) * GROUP, :])
+
+        def load_w(w):
+            for g in range(PASSES):
+                nc.sync.dma_start(out=w_raw[w][g][:], in_=w_views[w][g])
+
+        load_x(0)
+        load_w(0)
+        load_x(1)
+        load_w(1)
+        load_x(2)
+        load_x(3)
+
+        cols_ps = psum_t.tile([P, P], BF16, tag="xt")
+        nc.tensor.transpose(cols_ps[:], rows[:], ident_bf[:])
+        gb_cols = const.tile([P, 2 * CHUNKS], F32, name="gb_cols")
+        nc.vector.tensor_copy(out=gb_cols[:], in_=cols_ps[:, 0 : 2 * CHUNKS])
+        uv_cols = const.tile([P, 2 * HEADS], BF16, name="uv_cols")
+        nc.vector.tensor_copy(out=uv_cols[:], in_=cols_ps[:, 2 * CHUNKS : 2 * CHUNKS + 2 * HEADS])
+
+        def spread_biases():
+            for b in range(2 * HALVES):
+                bias_ps = psum_o.tile([P, N_TILE], F32, tag="acc")
+                for i in range(N_TILE // P):
+                    c = b * (N_TILE // P) + i
+                    nc.tensor.matmul(
+                        bias_ps[:, i * P : (i + 1) * P],
+                        lhsT=uv_cols[:, c : c + 1].to_broadcast([P, P]),
+                        rhs=ident_bf[:],
+                        start=True,
+                        stop=True,
+                    )
+                nc.scalar.copy(
+                    out=bias_all[:].rearrange("p b n -> p (b n)")[:, b * N_TILE : (b + 1) * N_TILE],
+                    in_=bias_ps[:],
+                )
+
+        bias_all = const.tile([P, 2, FEATURES], F32, name="bias_all")
+
+        h_codes = keep.tile([P, GROUPS * PASSES * GROUP_TOKENS], U32, name="h_codes", align_bytes=64)
+        h_scales = keep.tile([P, GROUPS * PASSES * GROUP_TOKENS], U8, name="h_scales", align_bytes=64)
+        w_codes = keep.tile([P, 2 * HALVES * PASSES * N_TILE], U32, name="w_codes", align_bytes=64)
+        w_scales = keep.tile([P, 2 * HALVES * PASSES * N_TILE], U8, name="w_scales", align_bytes=64)
+
+        def prepare_w(w, half, copies):
+            block = w * HALVES + half
+            w_grouped = work.tile([P, PASSES, N_TILE, PACK], BF16, tag="w_grouped", align_bytes=64)
+            for g in range(PASSES):
+                for c0 in range(0, N_TILE, W_PIECE):
+                    dst, src = regroup_views(
+                        w_grouped[:, g, c0 : c0 + W_PIECE, :],
+                        w_raw[w][g][:, :, half * N_TILE + c0 : half * N_TILE + c0 + W_PIECE],
+                    )
+                    copies[g](out=dst, in_=src)
+            cols = slice(block * PASSES * N_TILE, (block + 1) * PASSES * N_TILE)
+            nc.vector.quantize_mx(
+                out=w_codes[:, cols].bitcast(FP8X4),
+                scales=w_scales[:, cols],
+                in_=w_grouped[:].rearrange("p g n t -> p (g n t)"),
+            )
+
+        def prepare_h(grp):
+            mean_var = small.tile([P, GROUP, 2], F32, tag="mean_var")
+            for jj in range(GROUP):
+                stats = small.tile([P, D_MODEL // BN_WIDTH, 6], F32, tag="stats")
+                for s in range(D_MODEL // BN_WIDTH):
+                    nc.vector.bn_stats(
+                        out=stats[:, s, :], in_=x_sb[grp][:, jj, s * BN_WIDTH : (s + 1) * BN_WIDTH]
+                    )
+                nc.vector.bn_aggr(out=mean_var[:, jj, :], in_=stats[:].rearrange("p s v -> p (s v)"))
+            std = small.tile([P, GROUP], F32, tag="std")
+            nc.scalar.activation(out=std[:], in_=mean_var[:, :, 1], func=ACT.Sqrt, bias=eps[:, 0:1])
+            rstd = small.tile([P, GROUP], F32, tag="rstd")
+            nc.vector.reciprocal(out=rstd[:], in_=std[:])
+
+            normed = []
+            for jj in range(GROUP):
+                xn = work.tile([P, D_MODEL], F32, tag="xn", bufs=2 * GROUP)
+                nc.vector.tensor_scalar(
+                    out=xn[:],
+                    in0=x_sb[grp][:, jj, :],
+                    scalar1=mean_var[:, jj, 0:1],
+                    scalar2=rstd[:, jj : jj + 1],
+                    op0=ALU.subtract,
+                    op1=ALU.mult,
+                )
+                normed.append(xn)
+
+            h_planes = work.tile([P, CHUNKS, GROUP_TOKENS], BF16, tag="h_planes")
+            for pair in range(CHUNKS // 2):
+                xt = psum_t.tile([P, 2, GROUP_TOKENS], F32, tag="xt")
+                for cc in range(2):
+                    c = 2 * pair + cc
+                    for jj in range(GROUP):
+                        nc.tensor.transpose(
+                            xt[:, cc, jj * P : (jj + 1) * P], normed[jj][:, c * P : (c + 1) * P], ident[:]
+                        )
+                for cc in range(2):
+                    c = 2 * pair + cc
+                    nc.scalar.activation(
+                        out=h_planes[:, c, :],
+                        in_=xt[:, cc, :],
+                        func=ACT.Identity,
+                        scale=gb_cols[:, c : c + 1],
+                        bias=gb_cols[:, CHUNKS + c : CHUNKS + c + 1],
+                    )
+
+            h_grouped = work.tile([P, PASSES, GROUP_TOKENS, PACK], BF16, tag="h_grouped", align_bytes=64)
+            for g in range(PASSES):
+                dst, src = regroup_views(h_grouped[:, g, :, :], h_planes[:, g * PACK : (g + 1) * PACK, :])
+                nc.vector.tensor_copy(out=dst, in_=src)
+            cols = slice(grp * PASSES * GROUP_TOKENS, (grp + 1) * PASSES * GROUP_TOKENS)
+            nc.vector.quantize_mx(
+                out=h_codes[:, cols].bitcast(FP8X4),
+                scales=h_scales[:, cols],
+                in_=h_grouped[:].rearrange("p g r t -> p (g r t)"),
+            )
+
+        def project(j, block):
+            grp, jj = divmod(j, GROUP)
+            acc = psum_o.tile([P, N_TILE], F32, tag="acc")
+            for g in range(PASSES):
+                h_cols = slice(
+                    (grp * PASSES + g) * GROUP_TOKENS + jj * P, (grp * PASSES + g) * GROUP_TOKENS + (jj + 1) * P
+                )
+                w_cols = slice((block * PASSES + g) * N_TILE, (block * PASSES + g + 1) * N_TILE)
+                nc.tensor.matmul_mx(
+                    out=acc[:],
+                    lhsT=h_codes[:, h_cols].bitcast(FP8X4),
+                    lhsT_scale=h_scales[:, h_cols],
+                    rhs=w_codes[:, w_cols].bitcast(FP8X4),
+                    rhs_scale=w_scales[:, w_cols],
+                    start=(g == 0),
+                    stop=(g == PASSES - 1),
+                )
+            return acc
+
+        def queries(j):
+            biased = stage.tile([P, 2, FEATURES], F32, tag="biased")
+            keys = stage.tile([P, FEATURES], F32, tag="keys")
+            for half in range(HALVES):
+                cols = slice(half * N_TILE, (half + 1) * N_TILE)
+                acc = project(j, half)
+                nc.scalar.copy(out=keys[:, cols], in_=acc[:])
+                nc.vector.tensor_tensor(
+                    out=biased[:, :, cols],
+                    in0=acc[:].unsqueeze(1).to_broadcast([P, 2, N_TILE]),
+                    in1=bias_all[:, :, cols],
+                    op=ALU.add,
+                )
+            nc.sync.dma_start(out=out_views[2][:, j, :], in_=keys[:])
+            nc.sync.dma_start(out=out_views[0][:, j, :], in_=biased[:, 0, :])
+            nc.sync.dma_start(out=out_views[1][:, j, :], in_=biased[:, 1, :])
+
+        def values(j):
+            vals = stage.tile([P, FEATURES], F32, tag="vals")
+            for half in range(HALVES):
+                acc = project(j, HALVES + half)
+                nc.scalar.copy(out=vals[:, half * N_TILE : (half + 1) * N_TILE], in_=acc[:])
+            nc.sync.dma_start(out=out_views[3][:, j, :], in_=vals[:])
+
+        prepare_h(0)
+        spread_biases()
+        prepare_w(0, 0, (nc.scalar.copy, nc.vector.tensor_copy))
+        prepare_w(0, 1, (nc.scalar.copy, nc.vector.tensor_copy))
+        prepare_h(1)
+        queries(0)
+        queries(1)
+        prepare_w(1, 0, (nc.scalar.copy, nc.scalar.copy))
+        prepare_w(1, 1, (nc.scalar.copy, nc.scalar.copy))
+        prepare_h(2)
+        queries(2)
+        queries(3)
+        for j in range(4):
+            values(j)
+        prepare_h(3)
+        for j in range(4, TOKEN_TILES):
+            queries(j)
+            values(j)

@@ -227,21 +227,18 @@ def tile_multiheadattentiowithrpe_pa_kernel(
             return acc
 
         def queries(j):
-            biased = stage.tile([P, 2, FEATURES], F32, tag="biased")
             keys = stage.tile([P, FEATURES], F32, tag="keys")
+            qu = stage.tile([P, FEATURES], F32, tag="qu")
+            qv = stage.tile([P, FEATURES], F32, tag="qv")
             for half in range(HALVES):
                 cols = slice(half * N_TILE, (half + 1) * N_TILE)
                 acc = project(j, half)
                 nc.scalar.copy(out=keys[:, cols], in_=acc[:])
-                nc.vector.tensor_tensor(
-                    out=biased[:, :, cols],
-                    in0=acc[:].unsqueeze(1).to_broadcast([P, 2, N_TILE]),
-                    in1=bias_all[:, :, cols],
-                    op=ALU.add,
-                )
+                nc.vector.tensor_tensor(out=qu[:, cols], in0=acc[:], in1=bias_all[:, 0, cols], op=ALU.add)
+                nc.gpsimd.tensor_tensor(out=qv[:, cols], in0=keys[:, cols], in1=bias_all[:, 1, cols], op=ALU.add)
             nc.sync.dma_start(out=out_views[2][:, j, :], in_=keys[:])
-            nc.sync.dma_start(out=out_views[0][:, j, :], in_=biased[:, 0, :])
-            nc.sync.dma_start(out=out_views[1][:, j, :], in_=biased[:, 1, :])
+            nc.sync.dma_start(out=out_views[0][:, j, :], in_=qu[:])
+            nc.sync.dma_start(out=out_views[1][:, j, :], in_=qv[:])
 
         def values(j):
             vals = stage.tile([P, FEATURES], F32, tag="vals")
@@ -257,8 +254,8 @@ def tile_multiheadattentiowithrpe_pa_kernel(
         prepare_h(1)
         queries(0)
         queries(1)
-        prepare_w(1, 0, (nc.scalar.copy, nc.scalar.copy))
-        prepare_w(1, 1, (nc.scalar.copy, nc.scalar.copy))
+        prepare_w(1, 0, (nc.scalar.copy, nc.vector.tensor_copy))
+        prepare_w(1, 1, (nc.scalar.copy, nc.vector.tensor_copy))
         prepare_h(2)
         queries(2)
         queries(3)

@@ -60,6 +60,7 @@ def tile_multiheadattentiowithrpe_pa_kernel(
         stage = ctx.enter_context(tc.tile_pool(name="stage", bufs=3))
         psum_t = ctx.enter_context(tc.psum_pool(name="psum_t", bufs=3))
         psum_o = ctx.enter_context(tc.psum_pool(name="psum_o", bufs=5))
+        ctx.enter_context(tc.manual_schedule())
 
         ident = const.tile([P, P], F32, name="ident")
         make_identity(nc, ident[:])
@@ -68,15 +69,6 @@ def tile_multiheadattentiowithrpe_pa_kernel(
 
         rows = const.tile([P, P], BF16, name="rows")
         nc.vector.memset(rows[:], 0.0)
-        for i, vec in enumerate(
-            (
-                gamma.rearrange("(c p) -> c p", p=P),
-                beta.rearrange("(c p) -> c p", p=P),
-                u_bias,
-                v_bias,
-            )
-        ):
-            nc.sync.dma_start(out=rows[i * CHUNKS : (i + 1) * CHUNKS, :], in_=vec)
         eps = const.tile([P, 1], F32, name="eps")
         nc.vector.memset(eps[:], EPS)
         warm = const.tile([P, 1], F32, name="warm")
@@ -96,18 +88,29 @@ def tile_multiheadattentiowithrpe_pa_kernel(
                 nc.sync.dma_start(out=w_raw[w][g][:], in_=w_views[w][g])
 
         load_x(0)
+        for i, vec in enumerate(
+            (
+                gamma.rearrange("(c p) -> c p", p=P),
+                beta.rearrange("(c p) -> c p", p=P),
+                u_bias,
+                v_bias,
+            )
+        ):
+            nc.sync.dma_start(out=rows[i * CHUNKS : (i + 1) * CHUNKS, :], in_=vec)
         load_w(0)
         load_x(1)
         load_w(1)
         load_x(2)
         load_x(3)
 
-        cols_ps = psum_t.tile([P, P], BF16, tag="xt")
-        nc.tensor.transpose(cols_ps[:], rows[:], ident_bf[:])
         gb_cols = const.tile([P, 2 * CHUNKS], F32, name="gb_cols")
-        nc.vector.tensor_copy(out=gb_cols[:], in_=cols_ps[:, 0 : 2 * CHUNKS])
         uv_cols = const.tile([P, 2 * HEADS], BF16, name="uv_cols")
-        nc.vector.tensor_copy(out=uv_cols[:], in_=cols_ps[:, 2 * CHUNKS : 2 * CHUNKS + 2 * HEADS])
+
+        def rows_to_columns():
+            cols_ps = psum_t.tile([P, P], BF16, tag="xt")
+            nc.tensor.transpose(cols_ps[:], rows[:], ident_bf[:])
+            nc.vector.tensor_copy(out=gb_cols[:], in_=cols_ps[:, 0 : 2 * CHUNKS])
+            nc.vector.tensor_copy(out=uv_cols[:], in_=cols_ps[:, 2 * CHUNKS : 2 * CHUNKS + 2 * HEADS])
 
         def spread_biases():
             for b in range(2 * HALVES):
@@ -133,78 +136,108 @@ def tile_multiheadattentiowithrpe_pa_kernel(
         w_codes = keep.tile([P, 2 * HALVES * PASSES * N_TILE], U32, name="w_codes", align_bytes=64)
         w_scales = keep.tile([P, 2 * HALVES * PASSES * N_TILE], U8, name="w_scales", align_bytes=64)
 
-        def prepare_w(w, half, copies):
+        w_grouped = {}
+
+        def regroup_w(w, half, g, copy):
+            if g == 0:
+                w_grouped[(w, half)] = work.tile(
+                    [P, PASSES, N_TILE, PACK], BF16, name="w_grouped", tag="w_grouped", align_bytes=64
+                )
+            for c0 in range(0, N_TILE, W_PIECE):
+                dst, src = regroup_views(
+                    w_grouped[(w, half)][:, g, c0 : c0 + W_PIECE, :],
+                    w_raw[w][g][:, :, half * N_TILE + c0 : half * N_TILE + c0 + W_PIECE],
+                )
+                copy(out=dst, in_=src)
+
+        def quantise_w(w, half):
             block = w * HALVES + half
-            w_grouped = work.tile([P, PASSES, N_TILE, PACK], BF16, tag="w_grouped", align_bytes=64)
-            for g in range(PASSES):
-                for c0 in range(0, N_TILE, W_PIECE):
-                    dst, src = regroup_views(
-                        w_grouped[:, g, c0 : c0 + W_PIECE, :],
-                        w_raw[w][g][:, :, half * N_TILE + c0 : half * N_TILE + c0 + W_PIECE],
-                    )
-                    copies[g](out=dst, in_=src)
             cols = slice(block * PASSES * N_TILE, (block + 1) * PASSES * N_TILE)
             nc.vector.quantize_mx(
                 out=w_codes[:, cols].bitcast(FP8X4),
                 scales=w_scales[:, cols],
-                in_=w_grouped[:].rearrange("p g n t -> p (g n t)"),
+                in_=w_grouped[(w, half)][:].rearrange("p g n t -> p (g n t)"),
             )
 
-        def prepare_h(grp):
-            mean_var = small.tile([P, GROUP, 2], F32, tag="mean_var")
+        mean_var = {}
+        std = {}
+        rstd = {}
+        normed = {}
+        h_planes = {}
+
+        def token_statistics(grp):
+            mean_var[grp] = small.tile([P, GROUP, 2], F32, name="mean_var", tag="mean_var")
+            stats = small.tile([P, GROUP, D_MODEL // BN_WIDTH, 6], F32, tag="stats")
             for jj in range(GROUP):
-                stats = small.tile([P, D_MODEL // BN_WIDTH, 6], F32, tag="stats")
                 for s in range(D_MODEL // BN_WIDTH):
                     nc.vector.bn_stats(
-                        out=stats[:, s, :], in_=x_sb[grp][:, jj, s * BN_WIDTH : (s + 1) * BN_WIDTH]
+                        out=stats[:, jj, s, :], in_=x_sb[grp][:, jj, s * BN_WIDTH : (s + 1) * BN_WIDTH]
                     )
-                nc.vector.bn_aggr(out=mean_var[:, jj, :], in_=stats[:].rearrange("p s v -> p (s v)"))
-            std = small.tile([P, GROUP], F32, tag="std")
-            nc.scalar.activation(out=std[:], in_=mean_var[:, :, 1], func=ACT.Sqrt, bias=eps[:, 0:1])
-            rstd = small.tile([P, GROUP], F32, tag="rstd")
-            nc.vector.reciprocal(out=rstd[:], in_=std[:])
+            for jj in range(GROUP):
+                nc.vector.bn_aggr(
+                    out=mean_var[grp][:, jj, :], in_=stats[:, jj, :, :].rearrange("p s v -> p (s v)")
+                )
 
-            normed = []
+        def standard_deviation(grp):
+            std[grp] = small.tile([P, GROUP], F32, name="std", tag="std")
+            nc.scalar.activation(
+                out=std[grp][:], in_=mean_var[grp][:, :, 1], func=ACT.Sqrt, bias=eps[:, 0:1]
+            )
+
+        def normalise(grp):
+            rstd[grp] = small.tile([P, GROUP], F32, name="rstd", tag="rstd")
+            nc.vector.reciprocal(out=rstd[grp][:], in_=std[grp][:])
+            normed[grp] = []
             for jj in range(GROUP):
                 xn = work.tile([P, D_MODEL], F32, tag="xn", bufs=2 * GROUP)
                 nc.vector.tensor_scalar(
                     out=xn[:],
                     in0=x_sb[grp][:, jj, :],
-                    scalar1=mean_var[:, jj, 0:1],
-                    scalar2=rstd[:, jj : jj + 1],
+                    scalar1=mean_var[grp][:, jj, 0:1],
+                    scalar2=rstd[grp][:, jj : jj + 1],
                     op0=ALU.subtract,
                     op1=ALU.mult,
                 )
-                normed.append(xn)
+                normed[grp].append(xn)
 
-            h_planes = work.tile([P, CHUNKS, GROUP_TOKENS], BF16, tag="h_planes")
+        def transpose_and_scale(grp):
+            h_planes[grp] = work.tile([P, CHUNKS, GROUP_TOKENS], BF16, name="h_planes", tag="h_planes")
             for pair in range(CHUNKS // 2):
                 xt = psum_t.tile([P, 2, GROUP_TOKENS], F32, tag="xt")
                 for cc in range(2):
                     c = 2 * pair + cc
                     for jj in range(GROUP):
                         nc.tensor.transpose(
-                            xt[:, cc, jj * P : (jj + 1) * P], normed[jj][:, c * P : (c + 1) * P], ident[:]
+                            xt[:, cc, jj * P : (jj + 1) * P], normed[grp][jj][:, c * P : (c + 1) * P], ident[:]
                         )
                 for cc in range(2):
                     c = 2 * pair + cc
                     nc.scalar.activation(
-                        out=h_planes[:, c, :],
+                        out=h_planes[grp][:, c, :],
                         in_=xt[:, cc, :],
                         func=ACT.Identity,
                         scale=gb_cols[:, c : c + 1],
                         bias=gb_cols[:, CHUNKS + c : CHUNKS + c + 1],
                     )
 
-            h_grouped = work.tile([P, PASSES, GROUP_TOKENS, PACK], BF16, tag="h_grouped", align_bytes=64)
+        h_grouped = {}
+
+        def regroup_h(grp):
+            h_grouped[grp] = work.tile(
+                [P, PASSES, GROUP_TOKENS, PACK], BF16, name="h_grouped", tag="h_grouped", align_bytes=64
+            )
             for g in range(PASSES):
-                dst, src = regroup_views(h_grouped[:, g, :, :], h_planes[:, g * PACK : (g + 1) * PACK, :])
+                dst, src = regroup_views(
+                    h_grouped[grp][:, g, :, :], h_planes[grp][:, g * PACK : (g + 1) * PACK, :]
+                )
                 nc.vector.tensor_copy(out=dst, in_=src)
+
+        def quantise_h(grp):
             cols = slice(grp * PASSES * GROUP_TOKENS, (grp + 1) * PASSES * GROUP_TOKENS)
             nc.vector.quantize_mx(
                 out=h_codes[:, cols].bitcast(FP8X4),
                 scales=h_scales[:, cols],
-                in_=h_grouped[:].rearrange("p g r t -> p (g r t)"),
+                in_=h_grouped[grp][:].rearrange("p g r t -> p (g r t)"),
             )
 
         def project(j, block):
@@ -226,19 +259,28 @@ def tile_multiheadattentiowithrpe_pa_kernel(
                 )
             return acc
 
-        def queries(j):
+        def store_keys(j, banks):
             keys = stage.tile([P, FEATURES], F32, tag="keys")
-            qu = stage.tile([P, FEATURES], F32, tag="qu")
-            qv = stage.tile([P, FEATURES], F32, tag="qv")
             for half in range(HALVES):
-                cols = slice(half * N_TILE, (half + 1) * N_TILE)
-                acc = project(j, half)
-                nc.scalar.copy(out=keys[:, cols], in_=acc[:])
-                nc.vector.tensor_tensor(out=qu[:, cols], in0=acc[:], in1=bias_all[:, 0, cols], op=ALU.add)
-                nc.gpsimd.tensor_tensor(out=qv[:, cols], in0=keys[:, cols], in1=bias_all[:, 1, cols], op=ALU.add)
+                nc.scalar.copy(out=keys[:, half * N_TILE : (half + 1) * N_TILE], in_=banks[half][:])
             nc.sync.dma_start(out=out_views[2][:, j, :], in_=keys[:])
-            nc.sync.dma_start(out=out_views[0][:, j, :], in_=qu[:])
-            nc.sync.dma_start(out=out_views[1][:, j, :], in_=qv[:])
+
+        biased = {}
+
+        def add_biases(j, half, bank):
+            if half == 0:
+                biased[j] = stage.tile([P, 2, FEATURES], F32, name="biased", tag="biased")
+            cols = slice(half * N_TILE, (half + 1) * N_TILE)
+            nc.vector.tensor_tensor(
+                out=biased[j][:, :, cols],
+                in0=bank[:].unsqueeze(1).to_broadcast([P, 2, N_TILE]),
+                in1=bias_all[:, :, cols],
+                op=ALU.add,
+            )
+
+        def store_biased(j):
+            nc.sync.dma_start(out=out_views[0][:, j, :], in_=biased[j][:, 0, :])
+            nc.sync.dma_start(out=out_views[1][:, j, :], in_=biased[j][:, 1, :])
 
         def values(j):
             vals = stage.tile([P, FEATURES], F32, tag="vals")
@@ -247,21 +289,53 @@ def tile_multiheadattentiowithrpe_pa_kernel(
                 nc.scalar.copy(out=vals[:, half * N_TILE : (half + 1) * N_TILE], in_=acc[:])
             nc.sync.dma_start(out=out_views[3][:, j, :], in_=vals[:])
 
-        prepare_h(0)
+        def scalar_spare_time(slot):
+            if slot < HALVES * PASSES:
+                regroup_w(1, slot // PASSES, slot % PASSES, nc.scalar.copy)
+            else:
+                for j in range(GROUP * (slot - HALVES * PASSES), GROUP * (slot - HALVES * PASSES + 1)):
+                    if j < TOKEN_TILES:
+                        values(j)
+
+        token_statistics(0)
+        standard_deviation(0)
+        rows_to_columns()
+        regroup_w(0, 0, 0, nc.vector.tensor_copy)
+        normalise(0)
+        regroup_w(0, 1, 0, nc.scalar.copy)
+        transpose_and_scale(0)
         spread_biases()
-        prepare_w(0, 0, (nc.scalar.copy, nc.vector.tensor_copy))
-        prepare_w(0, 1, (nc.scalar.copy, nc.vector.tensor_copy))
-        prepare_h(1)
-        queries(0)
-        queries(1)
-        prepare_w(1, 0, (nc.scalar.copy, nc.vector.tensor_copy))
-        prepare_w(1, 1, (nc.scalar.copy, nc.vector.tensor_copy))
-        prepare_h(2)
-        queries(2)
-        queries(3)
-        for j in range(4):
-            values(j)
-        prepare_h(3)
-        for j in range(4, TOKEN_TILES):
-            queries(j)
-            values(j)
+        regroup_w(0, 0, 1, nc.vector.tensor_copy)
+        regroup_w(0, 1, 1, nc.vector.tensor_copy)
+        quantise_w(0, 0)
+        regroup_h(0)
+        quantise_w(0, 1)
+        quantise_h(0)
+        scalar_spare_time(0)
+
+        for grp in range(GROUPS):
+            first, second = GROUP * grp, GROUP * grp + 1
+            more = grp + 1 < GROUPS
+            banks = {j: [project(j, half) for half in range(HALVES)] for j in (first, second)}
+            if more:
+                token_statistics(grp + 1)
+            store_keys(first, banks[first])
+            add_biases(first, 0, banks[first][0])
+            if more:
+                standard_deviation(grp + 1)
+                normalise(grp + 1)
+            store_keys(second, banks[second])
+            scalar_spare_time(2 * grp + 1)
+            add_biases(first, 1, banks[first][1])
+            store_biased(first)
+            add_biases(second, 0, banks[second][0])
+            add_biases(second, 1, banks[second][1])
+            store_biased(second)
+            if more:
+                transpose_and_scale(grp + 1)
+            if grp < HALVES:
+                quantise_w(1, grp)
+            scalar_spare_time(2 * grp + 2)
+            if more:
+                regroup_h(grp + 1)
+                quantise_h(grp + 1)

from contextlib import ExitStack

import concourse.mybir as mybir
from concourse.masks import make_identity

F32 = mybir.dt.float32
BF16 = mybir.dt.bfloat16
U32 = mybir.dt.uint32
U8 = mybir.dt.uint8
I32 = mybir.dt.int32
FP8X4 = mybir.dt.float8_e4m3fn_x4
ACT = mybir.ActivationFunctionType
ALU = mybir.AluOpType

P = 128
PACK = 4
K_PASS = P * PACK
TOKENS = 1024
D_MODEL = 1024
FEATURES = 1024
PASSES = D_MODEL // K_PASS
CHUNKS = D_MODEL // P
TOKEN_TILES = TOKENS // P
GROUP = 2
GROUPS = TOKEN_TILES // GROUP
GROUP_TOKENS = GROUP * P
N_TILE = 512
HALVES = FEATURES // N_TILE
HEADS = 8
W_PIECE = 256
BN_WIDTH = 512
EPS = 1e-5

FLOPS = 2 * TOKENS * D_MODEL * 2 * FEATURES


def regroup_views(grouped, planes):
    dst = grouped.rearrange("p (c i) t -> p c t i", i=4)
    src = planes.rearrange("p t (c i) -> p c t i", i=4)
    return dst, src


def tile_multiheadattentiowithrpe_pa_kernel(
    tc, x, gamma, beta, Wq, Wv, u_bias, v_bias, out_0, out_1, out_2, out_3
):
    nc = tc.nc

    x_view = x.rearrange("i b d -> (i b) d").rearrange("(p j) d -> p j d", j=TOKEN_TILES)
    out_views = [
        o.rearrange("i b h f -> (i b) (h f)").rearrange("(p j) n -> p j n", j=TOKEN_TILES)
        for o in (out_0, out_1, out_2, out_3)
    ]
    w_views = [w.rearrange("(g t p) n -> g p t n", t=PACK, p=P) for w in (Wq, Wv)]

    with ExitStack() as ctx:
        const = ctx.enter_context(tc.tile_pool(name="const", bufs=1))
        keep = ctx.enter_context(tc.tile_pool(name="keep", bufs=1))
        small = ctx.enter_context(tc.tile_pool(name="small", bufs=4))
        work = ctx.enter_context(tc.tile_pool(name="work", bufs=2))
        stage = ctx.enter_context(tc.tile_pool(name="stage", bufs=3))
        psum_t = ctx.enter_context(tc.psum_pool(name="psum_t", bufs=3))
        psum_o = ctx.enter_context(tc.psum_pool(name="psum_o", bufs=5))
        ctx.enter_context(tc.manual_schedule())

        ident = const.tile([P, P], F32, name="ident")
        make_identity(nc, ident[:])
        ident_bf = const.tile([P, P], BF16, name="ident_bf")
        make_identity(nc, ident_bf[:])

        rows = const.tile([P, P], BF16, name="rows")
        nc.vector.memset(rows[:], 0.0)
        eps = const.tile([P, 1], F32, name="eps")
        nc.vector.memset(eps[:], EPS)
        warm = const.tile([P, 1], F32, name="warm")
        nc.scalar.activation(out=warm[:], in_=eps[:], func=ACT.Sqrt)

        x_sb = [keep.tile([P, GROUP, D_MODEL], BF16, name="x_sb%d" % grp) for grp in range(GROUPS)]
        w_raw = [
            [keep.tile([P, PACK, FEATURES], BF16, name="w_raw%d%d" % (w, g)) for g in range(PASSES)]
            for w in range(2)
        ]

        def load_x(grp):
            nc.sync.dma_start(out=x_sb[grp][:], in_=x_view[:, grp * GROUP : (grp + 1) * GROUP, :])

        def load_w(w):
            for g in range(PASSES):
                nc.sync.dma_start(out=w_raw[w][g][:], in_=w_views[w][g])

        load_x(0)
        for i, vec in enumerate(
            (
                gamma.rearrange("(c p) -> c p", p=P),
                beta.rearrange("(c p) -> c p", p=P),
                u_bias,
                v_bias,
            )
        ):
            nc.sync.dma_start(out=rows[i * CHUNKS : (i + 1) * CHUNKS, :], in_=vec)
        load_w(0)
        load_x(1)
        load_w(1)
        load_x(2)
        load_x(3)

        gb_cols = const.tile([P, 2 * CHUNKS], F32, name="gb_cols")
        uv_cols = const.tile([P, 2 * HEADS], BF16, name="uv_cols")

        def rows_to_columns():
            cols_ps = psum_t.tile([P, P], BF16, tag="xt")
            nc.tensor.transpose(cols_ps[:], rows[:], ident_bf[:])
            nc.vector.tensor_copy(out=gb_cols[:], in_=cols_ps[:, 0 : 2 * CHUNKS])
            nc.vector.tensor_copy(out=uv_cols[:], in_=cols_ps[:, 2 * CHUNKS : 2 * CHUNKS + 2 * HEADS])

        def spread_biases():
            for b in range(2 * HALVES):
                bias_ps = psum_o.tile([P, N_TILE], F32, tag="acc")
                for i in range(N_TILE // P):
                    c = b * (N_TILE // P) + i
                    nc.tensor.matmul(
                        bias_ps[:, i * P : (i + 1) * P],
                        lhsT=uv_cols[:, c : c + 1].to_broadcast([P, P]),
                        rhs=ident_bf[:],
                        start=True,
                        stop=True,
                    )
                nc.scalar.copy(
                    out=bias_all[:].rearrange("p b n -> p (b n)")[:, b * N_TILE : (b + 1) * N_TILE],
                    in_=bias_ps[:],
                )

        bias_all = const.tile([P, 2, FEATURES], F32, name="bias_all")

        h_codes = keep.tile([P, GROUPS * PASSES * GROUP_TOKENS], U32, name="h_codes", align_bytes=64)
        h_scales = keep.tile([P, GROUPS * PASSES * GROUP_TOKENS], U8, name="h_scales", align_bytes=64)
        w_codes = keep.tile([P, 2 * HALVES * PASSES * N_TILE], U32, name="w_codes", align_bytes=64)
        w_scales = keep.tile([P, 2 * HALVES * PASSES * N_TILE], U8, name="w_scales", align_bytes=64)

        w_grouped = {}

        def regroup_w(w, half, g, copy):
            if g == 0:
                w_grouped[(w, half)] = work.tile(
                    [P, PASSES, N_TILE, PACK], BF16, name="w_grouped", tag="w_grouped", align_bytes=64
                )
            for c0 in range(0, N_TILE, W_PIECE):
                dst, src = regroup_views(
                    w_grouped[(w, half)][:, g, c0 : c0 + W_PIECE, :],
                    w_raw[w][g][:, :, half * N_TILE + c0 : half * N_TILE + c0 + W_PIECE],
                )
                copy(out=dst, in_=src)

        def quantise_w(w, half):
            block = w * HALVES + half
            cols = slice(block * PASSES * N_TILE, (block + 1) * PASSES * N_TILE)
            nc.vector.quantize_mx(
                out=w_codes[:, cols].bitcast(FP8X4),
                scales=w_scales[:, cols],
                in_=w_grouped[(w, half)][:].rearrange("p g n t -> p (g n t)"),
            )

        mean_var = {}
        std = {}
        rstd = {}
        normed = {}
        h_planes = {}

        def token_statistics(grp):
            mean_var[grp] = small.tile([P, GROUP, 2], F32, name="mean_var", tag="mean_var")
            stats = small.tile([P, GROUP, D_MODEL // BN_WIDTH, 6], F32, tag="stats")
            for jj in range(GROUP):
                for s in range(D_MODEL // BN_WIDTH):
                    nc.vector.bn_stats(
                        out=stats[:, jj, s, :], in_=x_sb[grp][:, jj, s * BN_WIDTH : (s + 1) * BN_WIDTH]
                    )
            for jj in range(GROUP):
                nc.vector.bn_aggr(
                    out=mean_var[grp][:, jj, :], in_=stats[:, jj, :, :].rearrange("p s v -> p (s v)")
                )

        def standard_deviation(grp):
            std[grp] = small.tile([P, GROUP], F32, name="std", tag="std")
            nc.scalar.activation(
                out=std[grp][:], in_=mean_var[grp][:, :, 1], func=ACT.Sqrt, bias=eps[:, 0:1]
            )

        def normalise(grp):
            rstd[grp] = small.tile([P, GROUP], F32, name="rstd", tag="rstd")
            nc.vector.reciprocal(out=rstd[grp][:], in_=std[grp][:])
            normed[grp] = []
            for jj in range(GROUP):
                xn = work.tile([P, D_MODEL], F32, tag="xn", bufs=2 * GROUP)
                nc.vector.tensor_scalar(
                    out=xn[:],
                    in0=x_sb[grp][:, jj, :],
                    scalar1=mean_var[grp][:, jj, 0:1],
                    scalar2=rstd[grp][:, jj : jj + 1],
                    op0=ALU.subtract,
                    op1=ALU.mult,
                )
                normed[grp].append(xn)

        def transpose_and_scale(grp):
            h_planes[grp] = work.tile([P, CHUNKS, GROUP_TOKENS], BF16, name="h_planes", tag="h_planes")
            for pair in range(CHUNKS // 2):
                xt = psum_t.tile([P, 2, GROUP_TOKENS], F32, tag="xt")
                for cc in range(2):
                    c = 2 * pair + cc
                    for jj in range(GROUP):
                        nc.tensor.transpose(
                            xt[:, cc, jj * P : (jj + 1) * P], normed[grp][jj][:, c * P : (c + 1) * P], ident[:]
                        )
                for cc in range(2):
                    c = 2 * pair + cc
                    nc.scalar.activation(
                        out=h_planes[grp][:, c, :],
                        in_=xt[:, cc, :],
                        func=ACT.Identity,
                        scale=gb_cols[:, c : c + 1],
                        bias=gb_cols[:, CHUNKS + c : CHUNKS + c + 1],
                    )

        h_grouped = {}

        def regroup_h(grp):
            h_grouped[grp] = work.tile(
                [P, PASSES, GROUP_TOKENS, PACK], BF16, name="h_grouped", tag="h_grouped", align_bytes=64
            )
            for g in range(PASSES):
                dst, src = regroup_views(
                    h_grouped[grp][:, g, :, :], h_planes[grp][:, g * PACK : (g + 1) * PACK, :]
                )
                nc.vector.tensor_copy(out=dst, in_=src)

        def quantise_h(grp):
            cols = slice(grp * PASSES * GROUP_TOKENS, (grp + 1) * PASSES * GROUP_TOKENS)
            nc.vector.quantize_mx(
                out=h_codes[:, cols].bitcast(FP8X4),
                scales=h_scales[:, cols],
                in_=h_grouped[grp][:].rearrange("p g r t -> p (g r t)"),
            )

        def project(j, block):
            grp, jj = divmod(j, GROUP)
            acc = psum_o.tile([P, N_TILE], F32, tag="acc")
            for g in range(PASSES):
                h_cols = slice(
                    (grp * PASSES + g) * GROUP_TOKENS + jj * P, (grp * PASSES + g) * GROUP_TOKENS + (jj + 1) * P
                )
                w_cols = slice((block * PASSES + g) * N_TILE, (block * PASSES + g + 1) * N_TILE)
                nc.tensor.matmul_mx(
                    out=acc[:],
                    lhsT=h_codes[:, h_cols].bitcast(FP8X4),
                    lhsT_scale=h_scales[:, h_cols],
                    rhs=w_codes[:, w_cols].bitcast(FP8X4),
                    rhs_scale=w_scales[:, w_cols],
                    start=(g == 0),
                    stop=(g == PASSES - 1),
                )
            return acc

        def store_keys(j, banks):
            keys = stage.tile([P, FEATURES], F32, tag="keys")
            for half in range(HALVES):
                nc.scalar.copy(out=keys[:, half * N_TILE : (half + 1) * N_TILE], in_=banks[half][:])
            nc.sync.dma_start(out=out_views[2][:, j, :], in_=keys[:])

        biased = {}

        def add_biases(j, half, bank):
            if half == 0:
                biased[j] = stage.tile([P, 2, FEATURES], F32, name="biased", tag="biased")
            cols = slice(half * N_TILE, (half + 1) * N_TILE)
            nc.vector.tensor_tensor(
                out=biased[j][:, :, cols],
                in0=bank[:].unsqueeze(1).to_broadcast([P, 2, N_TILE]),
                in1=bias_all[:, :, cols],
                op=ALU.add,
            )

        def store_biased(j):
            nc.sync.dma_start(out=out_views[0][:, j, :], in_=biased[j][:, 0, :])
            nc.sync.dma_start(out=out_views[1][:, j, :], in_=biased[j][:, 1, :])

        def values(j):
            vals = stage.tile([P, FEATURES], F32, tag="vals")
            for half in range(HALVES):
                acc = project(j, HALVES + half)
                nc.scalar.copy(out=vals[:, half * N_TILE : (half + 1) * N_TILE], in_=acc[:])
            nc.sync.dma_start(out=out_views[3][:, j, :], in_=vals[:])

        def scalar_spare_time(slot):
            if slot < HALVES * PASSES:
                regroup_w(1, slot // PASSES, slot % PASSES, nc.scalar.copy)
            else:
                for j in range(GROUP * (slot - HALVES * PASSES), GROUP * (slot - HALVES * PASSES + 1)):
                    if j < TOKEN_TILES:
                        values(j)

        token_statistics(0)
        standard_deviation(0)
        rows_to_columns()
        regroup_w(0, 0, 0, nc.vector.tensor_copy)
        normalise(0)
        regroup_w(0, 1, 0, nc.scalar.copy)
        transpose_and_scale(0)
        spread_biases()
        regroup_w(0, 0, 1, nc.vector.tensor_copy)
        regroup_w(0, 1, 1, nc.vector.tensor_copy)
        quantise_w(0, 0)
        regroup_h(0)
        quantise_w(0, 1)
        quantise_h(0)
        scalar_spare_time(0)

        for grp in range(GROUPS):
            first, second = GROUP * grp, GROUP * grp + 1
            more = grp + 1 < GROUPS
            banks = {j: [project(j, half) for half in range(HALVES)] for j in (first, second)}
            if more:
                token_statistics(grp + 1)
            store_keys(first, banks[first])
            add_biases(first, 0, banks[first][0])
            if more:
                standard_deviation(grp + 1)
                normalise(grp + 1)
            store_keys(second, banks[second])
            scalar_spare_time(2 * grp + 1)
            add_biases(first, 1, banks[first][1])
            store_biased(first)
            add_biases(second, 0, banks[second][0])
            add_biases(second, 1, banks[second][1])
            store_biased(second)
            if more:
                transpose_and_scale(grp + 1)
            if grp < HALVES:
                quantise_w(1, grp)
            scalar_spare_time(2 * grp + 2)
            if more:
                regroup_h(grp + 1)
                quantise_h(grp + 1)
